import numpy as np
import ml_dtypes


def mxq(x, axis, fmt="e4m3"):
    dtype, down = {"e4m3": (ml_dtypes.float8_e4m3fn, 7), "e5m2": (ml_dtypes.float8_e5m2, 14)}[fmt]
    v = np.moveaxis(np.asarray(x, np.float32).astype(ml_dtypes.bfloat16).astype(np.float64), axis, -1)
    blocks = v.reshape(v.shape[:-1] + (-1, 32))
    amax = np.abs(blocks).max(-1, keepdims=True)
    byte = np.maximum(np.where(amax > 0, np.frexp(amax)[1] - 1 + 127, 0) - down, 1)
    scale = np.exp2(byte - 127.0)
    codes = (blocks / scale).astype(np.float32).astype(dtype).astype(np.float64)
    return np.moveaxis((codes * scale).reshape(v.shape), -1, axis)


WIDE = False


def mx_kscale(k):
    if not WIDE:
        return np.ones(k)
    levels = np.array([10, -10, 5, -5, 0])
    if k % 512:
        return np.exp2(np.random.permutation(np.resize(levels, k // 32))).repeat(32)
    a = np.empty((k // 512, 16))
    for p in range(k // 512):
        a[p, :8] = np.random.permutation(np.resize(levels, 8))
        for g in range(8):
            far = levels[np.abs(levels - a[p, g]) >= 10]
            a[p, g + 8] = far[np.random.randint(len(far))]
    return np.exp2(a.ravel()).repeat(32)


BF16 = ml_dtypes.bfloat16


def bf(x):
    return np.asarray(x, np.float32).astype(BF16)


def f64(x):
    return np.asarray(x).astype(np.float64)


B, IN_C, OUT_C, H, W, K, STRIDE, PAD = 128, 512, 128, 4, 4, 3, 1, 1
OH = (H + 2 * PAD - K) // STRIDE + 1
OW = (W + 2 * PAD - K) // STRIDE + 1


def _span(t, n_in, n_out):
    lo = max(0, -((t - PAD) // STRIDE))
    hi = min(n_out, (n_in - 1 + PAD - t) // STRIDE + 1)
    return lo, hi


def setup_inputs():
    s = mx_kscale(IN_C)
    x = np.random.standard_normal((B, IN_C, H, W)) * s[None, :, None, None]
    weights = np.random.uniform(0.0, 1.0, (OH, OW, OUT_C, IN_C, K, K)) * (1.7 / np.sqrt(IN_C * K * K)) / s[None, None, None, :, None, None]
    bias = np.random.uniform(0.0, 1.0, (OUT_C, OH, OW))
    return {"x": bf(x), "weights": bf(weights), "bias": bf(bias)}


def reference(x, weights, bias):
    xq = mxq(f64(x), 1, "e4m3")
    wf = f64(weights)
    acc = np.zeros((OH, OW, B, OUT_C))
    for i in range(K):
        h0, h1 = _span(i, H, OH)
        for j in range(K):
            w0, w1 = _span(j, W, OW)
            xs = xq[:, :, h0 * STRIDE + i - PAD:(h1 - 1) * STRIDE + i - PAD + 1:STRIDE,
                    w0 * STRIDE + j - PAD:(w1 - 1) * STRIDE + j - PAD + 1:STRIDE]
            wq = mxq(wf[h0:h1, w0:w1, :, :, i, j], 3, "e4m3")
            acc[h0:h1, w0:w1] += xs.transpose(2, 3, 0, 1) @ wq.transpose(0, 1, 3, 2)
    return acc.transpose(2, 3, 0, 1) + f64(bias)[None]

@@ -1,0 +1,281 @@
+from contextlib import ExitStack
+
+import concourse.mybir as mybir
+from concourse.masks import make_identity
+
+BF16 = mybir.dt.bfloat16
+F32 = mybir.dt.float32
+U32 = mybir.dt.uint32
+U8 = mybir.dt.uint8
+FP8X4 = mybir.dt.float8_e4m3fn_x4
+
+P = 128
+B = 128
+C = 512
+O = 128
+HW = 4
+KK = 3
+NPIX = HW * HW
+NTAP = KK * KK
+ROW = C * NTAP
+GROUP = 8
+XGROUP = 4
+FLOPS = 2 * 100 * B * O * C
+
+ROW_ORDER = (1, 2, 0, 3)
+COL_ORDER = (1, 2, 0, 3)
+LOAD_BUFS = 8
+D_BUFS = 5
+G_BUFS = 3
+Q_BUFS = 5
+TP_BUFS = 6
+ACT_EVERY = 4
+LOOKAHEAD = 1
+STORE_CUTS = 4
+W_FIRST = 2
+X_AT = 2
+X_ON_VECTOR = (1, 3, 5, 7)
+MANUAL = True
+
+
+def valid(p):
+    return [t for t in range(KK) if 0 <= p + t - 1 < HW]
+
+
+def tile_locallyconnected2d_kernel(tc, x, weights, bias, out):
+    nc = tc.nc
+    with ExitStack() as ctx:
+        if MANUAL:
+            ctx.enter_context(tc.manual_schedule())
+        const = ctx.enter_context(tc.tile_pool(name="const", bufs=1))
+        loads = ctx.enter_context(tc.tile_pool(name="loads", bufs=LOAD_BUFS))
+        dpool = ctx.enter_context(tc.tile_pool(name="dpool", bufs=D_BUFS))
+        gpool = ctx.enter_context(tc.tile_pool(name="gpool", bufs=G_BUFS))
+        qpool = ctx.enter_context(tc.tile_pool(name="qpool", bufs=Q_BUFS))
+        tpool = ctx.enter_context(tc.psum_pool(name="tpool", bufs=TP_BUFS))
+        apool = ctx.enter_context(tc.psum_pool(name="apool", bufs=2))
+
+        locs = [(h, w) for h in ROW_ORDER for w in COL_ORDER]
+
+        w_raw = {}
+        next_load = [0]
+
+        def load_next():
+            k = next_load[0]
+            if k < len(locs):
+                h, w = locs[k]
+                t = loads.tile([P, ROW], BF16, tag="ld", name="wraw%d" % k)
+                rows = weights[h, w].rearrange("o c i j -> o (c i j)")
+                if k == 0:
+                    for half in range(2):
+                        nc.sync.dma_start(
+                            out=t[:, half * ROW // 2 : (half + 1) * ROW // 2],
+                            in_=rows[:, half * ROW // 2 : (half + 1) * ROW // 2],
+                        )
+                else:
+                    nc.sync.dma_start(out=t[:], in_=rows)
+                w_raw[k] = t
+                next_load[0] += 1
+
+        for k in range(W_FIRST):
+            load_next()
+        x_tile = const.tile([P, C * NPIX], BF16, name="x_tile")
+        for u in range(2):
+            nc.sync.dma_start(
+                out=x_tile[:, 256 * NPIX * u : 256 * NPIX * (u + 1)],
+                in_=x[:, 256 * u : 256 * (u + 1)].rearrange("b c y x -> b (c y x)"),
+            )
+        for k in range(LOAD_BUFS - W_FIRST):
+            load_next()
+
+
+        ident = const.tile([P, P], F32, name="ident")
+        make_identity(nc, ident[:])
+        bias_all = const.tile([P, O * NPIX], BF16, name="bias_all")
+        nc.sync.dma_start(out=bias_all[:], in_=bias.rearrange("o y x -> (o y x)").partition_broadcast(P))
+        result = const.tile([P, O * NPIX], F32, name="result")
+        xq = const.tile([P, NPIX * B], U32, name="xq", align_bytes=64)
+        xs = const.tile([P, NPIX * B], U8, name="xs", align_bytes=64)
+
+        x32 = x_tile[:].bitcast(F32)
+        pending = []
+        n_xq = [0]
+
+        def quantise_x():
+            g, p0 = pending[n_xq[0]]
+            n_xq[0] += 1
+            nc.vector.quantize_mx(
+                out=xq[:, p0 : p0 + XGROUP * B].bitcast(FP8X4),
+                scales=xs[:, p0 : p0 + XGROUP * B],
+                in_=g[:],
+            )
+
+        def x_phase():
+            for quad in range(4):
+                g = gpool.tile([P, XGROUP * C], BF16, tag="g", name="gx%d" % quad, align_bytes=64)
+                for bk in range(2):
+                    rho = 2 * quad + bk
+                    ps = tpool.tile([P, 512], F32, tag="tp", name="px%d" % rho)
+                    for j in range(4):
+                        first = 8 * j + rho
+                        nc.tensor.transpose(
+                            ps[:, j * P : (j + 1) * P],
+                            x32[:, first : first + 32 * (P - 1) + 1 : 32],
+                            ident[:],
+                        )
+                    (nc.vector.tensor_copy if rho in X_ON_VECTOR else nc.scalar.copy)(
+                        out=g[:, 1024 * bk : 1024 * (bk + 1)].rearrange("p (e b j) -> p e b j", e=2, j=4),
+                        in_=ps[:].bitcast(BF16).rearrange("p (j b e) -> p e b j", j=4, e=2),
+                    )
+                pending.append((g, quad * XGROUP * B))
+                if len(pending) > 1:
+                    quantise_x()
+            quantise_x()
+
+        taps = []
+        for k, (h, w) in enumerate(locs):
+            lst = [(i, j) for i in valid(h) for j in valid(w)]
+            for s, (i, j) in enumerate(lst):
+                taps.append((k, h, w, i, j, s, s == 0, s == len(lst) - 1))
+        n_coarse = 80
+        groups = [taps[a : a + GROUP] for a in range(0, n_coarse, GROUP)]
+        groups += [taps[a : a + XGROUP] for a in range(n_coarse, len(taps), XGROUP)]
+        ng = len(groups)
+
+        counter = [0]
+
+        def deinterleave(dst, src):
+            counter[0] += 1
+            if counter[0] % ACT_EVERY == 0:
+                nc.scalar.copy(out=dst, in_=src)
+            else:
+                nc.vector.tensor_copy(out=dst, in_=src)
+
+        d32_of = {}
+
+        def s2(k):
+            h, w = locs[k]
+            js = valid(w)
+            rows_i = valid(h)
+            nj = len(js)
+            d = dpool.tile([P, ROW], BF16, tag="d", name="d%d" % k)
+            src = w_raw[k][:].rearrange("o (c i j) -> o c i j", i=KK, j=KK)
+            if k == 0:
+                for half in range(2):
+                    cs = slice(half * C // 2, (half + 1) * C // 2)
+                    for a, i in enumerate(rows_i):
+                        (nc.scalar.copy if a == 1 else nc.vector.tensor_copy)(
+                            out=d[:, a * nj * C : (a + 1) * nj * C].rearrange("o (s c) -> o c s", c=C)[:, cs, :],
+                            in_=src[:, cs, i, js[0] : js[0] + nj],
+                        )
+            else:
+                a = 0
+                while a < len(rows_i):
+                    ni = 2 if (nj == 2 and a + 1 < len(rows_i)) else 1
+                    if ni == 2:
+                        deinterleave(
+                            d[:, a * nj * C : (a + 2) * nj * C].rearrange("o (i j c) -> o c i j", i=2, j=2),
+                            src[:, :, rows_i[a] : rows_i[a] + 2, js[0] : js[0] + 2],
+                        )
+                    else:
+                        deinterleave(
+                            d[:, a * nj * C : (a + 1) * nj * C].rearrange("o (s c) -> o c s", c=C),
+                            src[:, :, rows_i[a], js[0] : js[0] + nj],
+                        )
+                    a += ni
+            load_next()
+            d32_of[k] = d[:].bitcast(F32)
+
+        done_s2 = [0]
+
+        def ensure_s2(upto):
+            while done_s2[0] <= upto:
+                s2(done_s2[0])
+                done_s2[0] += 1
+
+        g_of = {}
+        q_of = {}
+        acc_of = {}
+
+        def stage_t(gi):
+            grp = groups[gi]
+            g = gpool.tile([P, GROUP * C], BF16, tag="g", name="g%d" % gi, align_bytes=64)
+            g32 = g[:].bitcast(F32)
+            for bk in range(len(grp) // 2):
+                ps = tpool.tile([P, 512], F32, tag="tp", name="pw%d_%d" % (gi, bk))
+                for t in range(2):
+                    tap = grp[2 * bk + t]
+                    d32 = d32_of[tap[0]]
+                    for u in range(2):
+                        nc.tensor.transpose(
+                            ps[:, (2 * t + u) * P : (2 * t + u + 1) * P],
+                            d32[:, tap[5] * 256 + u : tap[5] * 256 + 256 : 2],
+                            ident[:],
+                        )
+                nc.scalar.copy(
+                    out=g32[:, 512 * bk : 512 * (bk + 1)].rearrange("p (t o u) -> p t o u", t=2, u=2),
+                    in_=ps[:].rearrange("p (t u o) -> p t o u", t=2, u=2),
+                )
+            g_of[gi] = g
+
+        def stage_q(gi):
+            wq = qpool.tile([P, GROUP * O], U32, tag="wq", name="wq%d" % gi, align_bytes=64)
+            ws = qpool.tile([P, GROUP * O], U8, tag="ws", name="ws%d" % gi, align_bytes=64)
+            n = len(groups[gi])
+            nc.vector.quantize_mx(
+                out=wq[:, 0 : n * O].bitcast(FP8X4), scales=ws[:, 0 : n * O], in_=g_of[gi][:, 0 : n * C]
+            )
+            q_of[gi] = (wq, ws)
+
+        res3 = result[:].rearrange("b (o l) -> b o l", l=NPIX)
+        bias3 = bias_all[:].rearrange("b (o l) -> b o l", l=NPIX)
+        out2 = out.rearrange("b o y x -> b (o y x)")
+
+        def finish_row(h, acc):
+            acc3 = acc[:].rearrange("b (w o) -> b o w", w=HW)
+            cuts = STORE_CUTS if h == ROW_ORDER[-1] else 1
+            step = O // cuts
+            for q in range(cuts):
+                nc.vector.tensor_tensor(
+                    out=res3[:, q * step : (q + 1) * step, HW * h : HW * (h + 1)],
+                    in0=acc3[:, q * step : (q + 1) * step, :],
+                    in1=bias3[:, q * step : (q + 1) * step, HW * h : HW * (h + 1)],
+                    op=mybir.AluOpType.add,
+                )
+                if h == ROW_ORDER[-1]:
+                    nc.sync.dma_start(
+                        out=out2[:, q * step * NPIX : (q + 1) * step * NPIX],
+                        in_=result[:, q * step * NPIX : (q + 1) * step * NPIX],
+                    )
+
+        def stage_m(gi):
+            wq, ws = q_of[gi]
+            for n, (k, h, w, i, j, s, first, last) in enumerate(groups[gi]):
+                if w == COL_ORDER[0] and first:
+                    acc_of[h] = apool.tile([P, 512], F32, tag="acc", name="acc%d" % h)
+                acc = acc_of[h]
+                pix = (h + i - 1) * HW + (w + j - 1)
+                nc.tensor.matmul_mx(
+                    out=acc[:, w * O : (w + 1) * O],
+                    lhsT=xq[:, pix * B : (pix + 1) * B].bitcast(FP8X4),
+                    lhsT_scale=xs[:, pix * B : (pix + 1) * B],
+                    rhs=wq[:, n * O : (n + 1) * O].bitcast(FP8X4),
+                    rhs_scale=ws[:, n * O : (n + 1) * O],
+                    start=first,
+                    stop=last,
+                )
+                if w == COL_ORDER[-1] and last:
+                    finish_row(h, acc)
+
+        m_done = [0]
+        for s in range(ng + 2):
+            if s == X_AT:
+                x_phase()
+            if s < ng:
+                ensure_s2(W_FIRST - 1 if s < X_AT else groups[min(s + LOOKAHEAD, ng - 1)][-1][0])
+                stage_t(s)
+            if 1 <= s <= ng:
+                stage_q(s - 1)
+            while s >= X_AT and m_done[0] <= s - 2:
+                stage_m(m_done[0])
+                m_done[0] += 1

@@ -19,23 +19,27 @@ NPIX = HW * HW
 NTAP = KK * KK
 ROW = C * NTAP
 GROUP = 8
+LAST_GROUP = 4
 XGROUP = 4
 FLOPS = 2 * 100 * B * O * C
 
 ROW_ORDER = (1, 2, 0, 3)
 COL_ORDER = (1, 2, 0, 3)
-LOAD_BUFS = 8
-D_BUFS = 5
-G_BUFS = 3
-Q_BUFS = 5
+LOAD_BUFS = 7
+D_BUFS = 6
+G_BUFS = 4
+Q_BUFS = 7
 TP_BUFS = 6
-ACT_EVERY = 4
-LOOKAHEAD = 1
 STORE_CUTS = 4
 W_FIRST = 2
-X_AT = 2
-X_ON_VECTOR = (1, 3, 5, 7)
-MANUAL = True
+X_AT = 6
+X_ON_VECTOR = ()
+LOOKAHEAD = 3
+PIECES = {0: 4, 1: 2}
+Q_LAG = 1
+XQ_LAG = 4
+X_STRIDE = 2
+M_LAG = 9
 
 
 def valid(p):
@@ -45,8 +49,7 @@ def valid(p):
 def tile_locallyconnected2d_kernel(tc, x, weights, bias, out):
     nc = tc.nc
     with ExitStack() as ctx:
-        if MANUAL:
-            ctx.enter_context(tc.manual_schedule())
+        ctx.enter_context(tc.manual_schedule())
         const = ctx.enter_context(tc.tile_pool(name="const", bufs=1))
         loads = ctx.enter_context(tc.tile_pool(name="loads", bufs=LOAD_BUFS))
         dpool = ctx.enter_context(tc.tile_pool(name="dpool", bufs=D_BUFS))
@@ -58,24 +61,18 @@ def tile_locallyconnected2d_kernel(tc, x, weights, bias, out):
         locs = [(h, w) for h in ROW_ORDER for w in COL_ORDER]
 
         w_raw = {}
-        next_load = [0]
 
         def load_next():
-            k = next_load[0]
+            k = len(w_raw)
             if k < len(locs):
                 h, w = locs[k]
                 t = loads.tile([P, ROW], BF16, tag="ld", name="wraw%d" % k)
                 rows = weights[h, w].rearrange("o c i j -> o (c i j)")
-                if k == 0:
-                    for half in range(2):
-                        nc.sync.dma_start(
-                            out=t[:, half * ROW // 2 : (half + 1) * ROW // 2],
-                            in_=rows[:, half * ROW // 2 : (half + 1) * ROW // 2],
-                        )
-                else:
-                    nc.sync.dma_start(out=t[:], in_=rows)
+                n = PIECES.get(k, 1)
+                for q in range(n):
+                    cols = slice(q * ROW // n, (q + 1) * ROW // n)
+                    nc.sync.dma_start(out=t[:, cols], in_=rows[:, cols])
                 w_raw[k] = t
-                next_load[0] += 1
 
         for k in range(W_FIRST):
             load_next()
@@ -88,7 +85,6 @@ def tile_locallyconnected2d_kernel(tc, x, weights, bias, out):
         for k in range(LOAD_BUFS - W_FIRST):
             load_next()
 
-
         ident = const.tile([P, P], F32, name="ident")
         make_identity(nc, ident[:])
         bias_all = const.tile([P, O * NPIX], BF16, name="bias_all")
@@ -98,125 +94,120 @@ def tile_locallyconnected2d_kernel(tc, x, weights, bias, out):
         xs = const.tile([P, NPIX * B], U8, name="xs", align_bytes=64)
 
         x32 = x_tile[:].bitcast(F32)
-        pending = []
-        n_xq = [0]
+        gx_of = {}
 
-        def quantise_x():
-            g, p0 = pending[n_xq[0]]
-            n_xq[0] += 1
+        def quantise_x(quad):
+            p0 = quad * XGROUP * B
             nc.vector.quantize_mx(
                 out=xq[:, p0 : p0 + XGROUP * B].bitcast(FP8X4),
                 scales=xs[:, p0 : p0 + XGROUP * B],
-                in_=g[:],
+                in_=gx_of[quad][:, 0 : XGROUP * C],
             )
 
-        def x_phase():
-            for quad in range(4):
-                g = gpool.tile([P, XGROUP * C], BF16, tag="g", name="gx%d" % quad, align_bytes=64)
-                for bk in range(2):
-                    rho = 2 * quad + bk
-                    ps = tpool.tile([P, 512], F32, tag="tp", name="px%d" % rho)
-                    for j in range(4):
-                        first = 8 * j + rho
-                        nc.tensor.transpose(
-                            ps[:, j * P : (j + 1) * P],
-                            x32[:, first : first + 32 * (P - 1) + 1 : 32],
-                            ident[:],
-                        )
-                    (nc.vector.tensor_copy if rho in X_ON_VECTOR else nc.scalar.copy)(
-                        out=g[:, 1024 * bk : 1024 * (bk + 1)].rearrange("p (e b j) -> p e b j", e=2, j=4),
-                        in_=ps[:].bitcast(BF16).rearrange("p (j b e) -> p e b j", j=4, e=2),
-                    )
-                pending.append((g, quad * XGROUP * B))
-                if len(pending) > 1:
-                    quantise_x()
-            quantise_x()
+        def x_bank(rho):
+            quad, bk = divmod(rho, 2)
+            if bk == 0:
+                gx_of[quad] = gpool.tile([P, GROUP * C], BF16, tag="g", name="gx%d" % quad, align_bytes=64)
+            ps = tpool.tile([P, 512], F32, tag="tp", name="px%d" % rho)
+            for t in range(4):
+                first = 8 * t + rho
+                nc.tensor.transpose(
+                    ps[:, t * P : (t + 1) * P],
+                    x32[:, first : first + 32 * (P - 1) + 1 : 32],
+                    ident[:],
+                )
+            (nc.vector.tensor_copy if rho in X_ON_VECTOR else nc.scalar.copy)(
+                out=gx_of[quad][:, 1024 * bk : 1024 * (bk + 1)].rearrange("p (e b j) -> p e b j", e=2, j=4),
+                in_=ps[:].bitcast(BF16).rearrange("p (j b e) -> p e b j", j=4, e=2),
+            )
 
         taps = []
         for k, (h, w) in enumerate(locs):
             lst = [(i, j) for i in valid(h) for j in valid(w)]
             for s, (i, j) in enumerate(lst):
                 taps.append((k, h, w, i, j, s, s == 0, s == len(lst) - 1))
-        n_coarse = 80
+        n_coarse = 88
         groups = [taps[a : a + GROUP] for a in range(0, n_coarse, GROUP)]
-        groups += [taps[a : a + XGROUP] for a in range(n_coarse, len(taps), XGROUP)]
+        groups += [taps[a : a + LAST_GROUP] for a in range(n_coarse, len(taps), LAST_GROUP)]
         ng = len(groups)
 
-        counter = [0]
+        on_scalar = lambda k, n: k != 0 and (n % 3 == 2 and k > 6) or (k == 0 and jobs[n][1] == 1)
+        copy_on_vector = lambda n: False
+        jobs = []
+        for k, (h, w) in enumerate(locs):
+            rows_i = valid(h)
+            nj = len(valid(w))
+            n = PIECES.get(k, 1)
+            step = 2 if nj == 2 else 1
+            for q in range(n):
+                for a in range(0, len(rows_i), step):
+                    jobs.append((k, a, min(step, len(rows_i) - a), q, n))
+        first_tap = [0]
+        for h, w in locs:
+            first_tap.append(first_tap[-1] + len(valid(h)) * len(valid(w)))
+        d_of = {}
+        done_jobs = [0]
 
-        def deinterleave(dst, src):
-            counter[0] += 1
-            if counter[0] % ACT_EVERY == 0:
+        def sort_next():
+            n = done_jobs[0]
+            k, a, ni, q, pieces = jobs[n]
+            h, w = locs[k]
+            i0, j0, nj = valid(h)[a], valid(w)[0], len(valid(w))
+            if k not in d_of:
+                d_of[k] = dpool.tile([P, ROW], BF16, tag="d", name="d%d" % k)
+            cs = slice(q * C // pieces, (q + 1) * C // pieces)
+            src = w_raw[k][:].rearrange("o (c i j) -> o c i j", i=KK, j=KK)
+            out_cols = d_of[k][:, a * nj * C : (a + ni) * nj * C]
+            if ni == 2:
+                dst = out_cols.rearrange("o (i j c) -> o c i j", i=2, j=2)[:, cs]
+                src = src[:, cs, i0 : i0 + 2, j0 : j0 + 2]
+            else:
+                dst = out_cols.rearrange("o (s c) -> o c s", c=C)[:, cs]
+                src = src[:, cs, i0, j0 : j0 + nj]
+            if on_scalar(k, n):
                 nc.scalar.copy(out=dst, in_=src)
             else:
                 nc.vector.tensor_copy(out=dst, in_=src)
+            done_jobs[0] += 1
+            if done_jobs[0] == len(jobs) or jobs[done_jobs[0]][0] != k:
+                load_next()
 
-        d32_of = {}
-
-        def s2(k):
-            h, w = locs[k]
-            js = valid(w)
-            rows_i = valid(h)
-            nj = len(js)
-            d = dpool.tile([P, ROW], BF16, tag="d", name="d%d" % k)
-            src = w_raw[k][:].rearrange("o (c i j) -> o c i j", i=KK, j=KK)
-            if k == 0:
-                for half in range(2):
-                    cs = slice(half * C // 2, (half + 1) * C // 2)
-                    for a, i in enumerate(rows_i):
-                        (nc.scalar.copy if a == 1 else nc.vector.tensor_copy)(
-                            out=d[:, a * nj * C : (a + 1) * nj * C].rearrange("o (s c) -> o c s", c=C)[:, cs, :],
-                            in_=src[:, cs, i, js[0] : js[0] + nj],
-                        )
-            else:
-                a = 0
-                while a < len(rows_i):
-                    ni = 2 if (nj == 2 and a + 1 < len(rows_i)) else 1
-                    if ni == 2:
-                        deinterleave(
-                            d[:, a * nj * C : (a + 2) * nj * C].rearrange("o (i j c) -> o c i j", i=2, j=2),
-                            src[:, :, rows_i[a] : rows_i[a] + 2, js[0] : js[0] + 2],
-                        )
-                    else:
-                        deinterleave(
-                            d[:, a * nj * C : (a + 1) * nj * C].rearrange("o (s c) -> o c s", c=C),
-                            src[:, :, rows_i[a], js[0] : js[0] + nj],
-                        )
-                    a += ni
-            load_next()
-            d32_of[k] = d[:].bitcast(F32)
-
-        done_s2 = [0]
-
-        def ensure_s2(upto):
-            while done_s2[0] <= upto:
-                s2(done_s2[0])
-                done_s2[0] += 1
+        def sort_up_to(tap, bank):
+            while done_jobs[0] < len(jobs):
+                k, a, ni, q, pieces = jobs[done_jobs[0]]
+                if first_tap[k] + a * len(valid(locs[k][1])) >= tap:
+                    break
+                if k >= D_BUFS and first_tap[k - D_BUFS + 1] > 2 * bank:
+                    break
+                sort_next()
 
         g_of = {}
         q_of = {}
         acc_of = {}
-
-        def stage_t(gi):
-            grp = groups[gi]
-            g = gpool.tile([P, GROUP * C], BF16, tag="g", name="g%d" % gi, align_bytes=64)
-            g32 = g[:].bitcast(F32)
+        group_of_bank = []
+        for gi, grp in enumerate(groups):
             for bk in range(len(grp) // 2):
-                ps = tpool.tile([P, 512], F32, tag="tp", name="pw%d_%d" % (gi, bk))
-                for t in range(2):
-                    tap = grp[2 * bk + t]
-                    d32 = d32_of[tap[0]]
-                    for u in range(2):
-                        nc.tensor.transpose(
-                            ps[:, (2 * t + u) * P : (2 * t + u + 1) * P],
-                            d32[:, tap[5] * 256 + u : tap[5] * 256 + 256 : 2],
-                            ident[:],
-                        )
-                nc.scalar.copy(
-                    out=g32[:, 512 * bk : 512 * (bk + 1)].rearrange("p (t o u) -> p t o u", t=2, u=2),
-                    in_=ps[:].rearrange("p (t u o) -> p t o u", t=2, u=2),
-                )
-            g_of[gi] = g
+                group_of_bank.append((gi, bk))
+
+        def w_bank(b):
+            gi, bk = group_of_bank[b]
+            grp = groups[gi]
+            if bk == 0:
+                g_of[gi] = gpool.tile([P, GROUP * C], BF16, tag="g", name="g%d" % gi, align_bytes=64)
+            ps = tpool.tile([P, 512], F32, tag="tp", name="pw%d_%d" % (gi, bk))
+            for t in range(2):
+                tap = grp[2 * bk + t]
+                d32 = d_of[tap[0]][:].bitcast(F32)
+                for u in range(2):
+                    nc.tensor.transpose(
+                        ps[:, (2 * t + u) * P : (2 * t + u + 1) * P],
+                        d32[:, tap[5] * 256 + u : tap[5] * 256 + 256 : 2],
+                        ident[:],
+                    )
+            (nc.vector.tensor_copy if copy_on_vector(b) else nc.scalar.copy)(
+                out=g_of[gi][:].bitcast(F32)[:, 512 * bk : 512 * (bk + 1)].rearrange("p (t o u) -> p t o u", t=2, u=2),
+                in_=ps[:].rearrange("p (t u o) -> p t o u", t=2, u=2),
+            )
 
         def stage_q(gi):
             wq = qpool.tile([P, GROUP * O], U32, tag="wq", name="wq%d" % gi, align_bytes=64)
@@ -267,15 +258,44 @@ def tile_locallyconnected2d_kernel(tc, x, weights, bias, out):
                 if w == COL_ORDER[-1] and last:
                     finish_row(h, acc)
 
-        m_done = [0]
-        for s in range(ng + 2):
-            if s == X_AT:
-                x_phase()
-            if s < ng:
-                ensure_s2(W_FIRST - 1 if s < X_AT else groups[min(s + LOOKAHEAD, ng - 1)][-1][0])
-                stage_t(s)
-            if 1 <= s <= ng:
-                stage_q(s - 1)
-            while s >= X_AT and m_done[0] <= s - 2:
-                stage_m(m_done[0])
-                m_done[0] += 1
+        nb = len(group_of_bank)
+        steps = []
+        for b in range(nb):
+            for r in range(2 * NPIX // XGROUP):
+                if b == X_AT + r * X_STRIDE:
+                    steps.append(("x", r))
+            steps.append(("w", b))
+        due_q = []
+        due_m = []
+        x_ready = False
+        t = 0
+        b = 0
+        extra = 0
+        while t < len(steps) or due_q or due_m:
+            if t < len(steps):
+                kind, n = steps[t]
+                if kind == "w":
+                    b = n
+                else:
+                    extra += 1
+                sort_up_to(2 * (b + 1 + LOOKAHEAD) + extra, b)
+                if kind == "w":
+                    w_bank(n)
+                    gi, bk = group_of_bank[n]
+                    if 2 * bk + 2 == len(groups[gi]):
+                        due_q.append((t + Q_LAG, "w", gi))
+                        due_m.append((t + M_LAG, gi))
+                else:
+                    x_bank(n)
+                    if n % 2 == 1:
+                        due_q.append((t + XQ_LAG, "x", n // 2))
+            for job in sorted(due_q):
+                if job[0] <= t:
+                    due_q.remove(job)
+                    fn = stage_q if job[1] == "w" else quantise_x
+                    fn(job[2])
+                    if job[1] == "x" and job[2] == NPIX // XGROUP - 1:
+                        x_ready = True
+            while due_m and due_m[0][0] <= t and x_ready:
+                stage_m(due_m.pop(0)[1])
+            t += 1

@@ -16,30 +16,29 @@ O = 128
 HW = 4
 KK = 3
 NPIX = HW * HW
-NTAP = KK * KK
-ROW = C * NTAP
-GROUP = 8
-LAST_GROUP = 4
-XGROUP = 4
+ROW = C * KK * KK
 FLOPS = 2 * 100 * B * O * C
 
 ROW_ORDER = (1, 2, 0, 3)
 COL_ORDER = (1, 2, 0, 3)
-LOAD_BUFS = 7
-D_BUFS = 6
-G_BUFS = 4
-Q_BUFS = 7
-TP_BUFS = 6
-STORE_CUTS = 4
-W_FIRST = 2
-X_AT = 6
-X_ON_VECTOR = ()
-LOOKAHEAD = 3
-PIECES = {0: 4, 1: 2}
+GROUP = 8
+LAST_GROUP = 4
+N_COARSE = 72
+XGROUP = 4
+W_FIRST = 1
+X_AT = 4
+X_STRIDE = 0
+PIECES = {0: 2}
+LOOKAHEAD = 4
 Q_LAG = 1
 XQ_LAG = 4
-X_STRIDE = 2
-M_LAG = 9
+M_LAG = 8
+LOAD_BUFS = 7
+D_BUFS = 7
+G_BUFS = 4
+Q_BUFS = 6
+TP_BUFS = 6
+STORE_CUTS = 4
 
 
 def valid(p):
@@ -59,30 +58,29 @@ def tile_locallyconnected2d_kernel(tc, x, weights, bias, out):
         apool = ctx.enter_context(tc.psum_pool(name="apool", bufs=2))
 
         locs = [(h, w) for h in ROW_ORDER for w in COL_ORDER]
-
-        w_raw = {}
+        order = [("w", k) for k in range(W_FIRST)] + [("x", 0), ("x", 1)] + [("w", k) for k in range(W_FIRST, len(locs))]
+        raw = {}
 
         def load_next():
-            k = len(w_raw)
-            if k < len(locs):
-                h, w = locs[k]
-                t = loads.tile([P, ROW], BF16, tag="ld", name="wraw%d" % k)
-                rows = weights[h, w].rearrange("o c i j -> o (c i j)")
-                n = PIECES.get(k, 1)
-                for q in range(n):
-                    cols = slice(q * ROW // n, (q + 1) * ROW // n)
-                    nc.sync.dma_start(out=t[:, cols], in_=rows[:, cols])
-                w_raw[k] = t
+            if len(raw) < len(order):
+                unit = order[len(raw)]
+                kind, k = unit
+                t = loads.tile([P, ROW], BF16, tag="ld", name="raw_%s%d" % unit)
+                if kind == "x":
+                    nc.sync.dma_start(
+                        out=t[:, 0 : C // 2 * NPIX],
+                        in_=x[:, C // 2 * k : C // 2 * (k + 1)].rearrange("b c y x -> b (c y x)"),
+                    )
+                else:
+                    h, w = locs[k]
+                    rows = weights[h, w].rearrange("o c i j -> o (c i j)")
+                    n = PIECES.get(k, 1)
+                    for q in range(n):
+                        cols = slice(q * ROW // n, (q + 1) * ROW // n)
+                        nc.sync.dma_start(out=t[:, cols], in_=rows[:, cols])
+                raw[unit] = t
 
-        for k in range(W_FIRST):
-            load_next()
-        x_tile = const.tile([P, C * NPIX], BF16, name="x_tile")
-        for u in range(2):
-            nc.sync.dma_start(
-                out=x_tile[:, 256 * NPIX * u : 256 * NPIX * (u + 1)],
-                in_=x[:, 256 * u : 256 * (u + 1)].rearrange("b c y x -> b (c y x)"),
-            )
-        for k in range(LOAD_BUFS - W_FIRST):
+        for n in range(LOAD_BUFS):
             load_next()
 
         ident = const.tile([P, P], F32, name="ident")
@@ -93,128 +91,131 @@ def tile_locallyconnected2d_kernel(tc, x, weights, bias, out):
         xq = const.tile([P, NPIX * B], U32, name="xq", align_bytes=64)
         xs = const.tile([P, NPIX * B], U8, name="xs", align_bytes=64)
 
-        x32 = x_tile[:].bitcast(F32)
-        gx_of = {}
-
-        def quantise_x(quad):
-            p0 = quad * XGROUP * B
-            nc.vector.quantize_mx(
-                out=xq[:, p0 : p0 + XGROUP * B].bitcast(FP8X4),
-                scales=xs[:, p0 : p0 + XGROUP * B],
-                in_=gx_of[quad][:, 0 : XGROUP * C],
-            )
-
-        def x_bank(rho):
-            quad, bk = divmod(rho, 2)
-            if bk == 0:
-                gx_of[quad] = gpool.tile([P, GROUP * C], BF16, tag="g", name="gx%d" % quad, align_bytes=64)
-            ps = tpool.tile([P, 512], F32, tag="tp", name="px%d" % rho)
-            for t in range(4):
-                first = 8 * t + rho
-                nc.tensor.transpose(
-                    ps[:, t * P : (t + 1) * P],
-                    x32[:, first : first + 32 * (P - 1) + 1 : 32],
-                    ident[:],
-                )
-            (nc.vector.tensor_copy if rho in X_ON_VECTOR else nc.scalar.copy)(
-                out=gx_of[quad][:, 1024 * bk : 1024 * (bk + 1)].rearrange("p (e b j) -> p e b j", e=2, j=4),
-                in_=ps[:].bitcast(BF16).rearrange("p (j b e) -> p e b j", j=4, e=2),
-            )
-
         taps = []
         for k, (h, w) in enumerate(locs):
             lst = [(i, j) for i in valid(h) for j in valid(w)]
             for s, (i, j) in enumerate(lst):
                 taps.append((k, h, w, i, j, s, s == 0, s == len(lst) - 1))
-        n_coarse = 88
-        groups = [taps[a : a + GROUP] for a in range(0, n_coarse, GROUP)]
-        groups += [taps[a : a + LAST_GROUP] for a in range(n_coarse, len(taps), LAST_GROUP)]
-        ng = len(groups)
+        groups = [taps[a : a + GROUP] for a in range(0, N_COARSE, GROUP)]
+        groups += [taps[a : a + LAST_GROUP] for a in range(N_COARSE, len(taps), LAST_GROUP)]
+        banks = [(gi, bk) for gi, grp in enumerate(groups) for bk in range(len(grp) // 2)]
+        n_xbanks = NPIX // 2
+        steps = []
+        for b in range(len(banks)):
+            for r in range(n_xbanks):
+                if b == X_AT + r * X_STRIDE:
+                    steps.append(("x", r))
+            steps.append(("w", b))
 
-        on_scalar = lambda k, n: k != 0 and (n % 3 == 2 and k > 6) or (k == 0 and jobs[n][1] == 1)
-        copy_on_vector = lambda n: False
+        first_use = {}
+        last_use = {}
+        for at, (kind, n) in enumerate(steps):
+            if kind == "x":
+                units = [("x", n // (n_xbanks // 2))]
+            else:
+                gi, bk = banks[n]
+                units = [("w", tap[0]) for tap in groups[gi][2 * bk : 2 * bk + 2]]
+            for unit in units:
+                first_use.setdefault(unit, at)
+                last_use[unit] = at
+
         jobs = []
-        for k, (h, w) in enumerate(locs):
-            rows_i = valid(h)
-            nj = len(valid(w))
-            n = PIECES.get(k, 1)
-            step = 2 if nj == 2 else 1
-            for q in range(n):
-                for a in range(0, len(rows_i), step):
-                    jobs.append((k, a, min(step, len(rows_i) - a), q, n))
-        first_tap = [0]
-        for h, w in locs:
-            first_tap.append(first_tap[-1] + len(valid(h)) * len(valid(w)))
+        for kind, k in order:
+            if kind == "x":
+                for quad in range(4):
+                    jobs.append(("x", k, quad, 4, 0, 1))
+            else:
+                rows_i, nj = valid(locs[k][0]), len(valid(locs[k][1]))
+                ni = 2 if nj == 2 else 1
+                n = PIECES.get(k, 1)
+                for q in range(n):
+                    for a in range(0, len(rows_i), ni):
+                        jobs.append(("w", k, a, min(ni, len(rows_i) - a), q, n))
+
+        def need(job):
+            kind, k, a, ni, q, n = job
+            return first_use[("x", a // 2) if kind == "x" else ("w", k)]
+
         d_of = {}
+        d_units = []
+
+        def sorted_tile(unit, at):
+            if unit not in d_of:
+                if len(d_units) >= D_BUFS and last_use[d_units[len(d_units) - D_BUFS]] >= at:
+                    return None
+                d_of[unit] = dpool.tile([P, ROW], BF16, tag="d", name="d_%s%d" % unit)
+                d_units.append(unit)
+            return d_of[unit]
+
         done_jobs = [0]
 
-        def sort_next():
-            n = done_jobs[0]
-            k, a, ni, q, pieces = jobs[n]
-            h, w = locs[k]
-            i0, j0, nj = valid(h)[a], valid(w)[0], len(valid(w))
-            if k not in d_of:
-                d_of[k] = dpool.tile([P, ROW], BF16, tag="d", name="d%d" % k)
-            cs = slice(q * C // pieces, (q + 1) * C // pieces)
-            src = w_raw[k][:].rearrange("o (c i j) -> o c i j", i=KK, j=KK)
-            out_cols = d_of[k][:, a * nj * C : (a + ni) * nj * C]
-            if ni == 2:
-                dst = out_cols.rearrange("o (i j c) -> o c i j", i=2, j=2)[:, cs]
-                src = src[:, cs, i0 : i0 + 2, j0 : j0 + 2]
-            else:
-                dst = out_cols.rearrange("o (s c) -> o c s", c=C)[:, cs]
-                src = src[:, cs, i0, j0 : j0 + nj]
-            if on_scalar(k, n):
-                nc.scalar.copy(out=dst, in_=src)
-            else:
-                nc.vector.tensor_copy(out=dst, in_=src)
-            done_jobs[0] += 1
-            if done_jobs[0] == len(jobs) or jobs[done_jobs[0]][0] != k:
-                load_next()
-
-        def sort_up_to(tap, bank):
+        def sort_up_to(limit, at):
             while done_jobs[0] < len(jobs):
-                k, a, ni, q, pieces = jobs[done_jobs[0]]
-                if first_tap[k] + a * len(valid(locs[k][1])) >= tap:
-                    break
-                if k >= D_BUFS and first_tap[k - D_BUFS + 1] > 2 * bank:
-                    break
-                sort_next()
+                n = done_jobs[0]
+                if min(need(job) for job in jobs[n:]) > limit:
+                    return
+                kind, k, a, ni, q, pieces = jobs[n]
+                unit = ("x", a // 2) if kind == "x" else ("w", k)
+                d = sorted_tile(unit, at)
+                if d is None:
+                    return
+                if kind == "x":
+                    dst = d[:, 4 * C * (a % 2) : 4 * C * (a % 2 + 1)].rearrange("b (l c) -> b c l", c=C)
+                    dst = dst[:, C // 2 * k : C // 2 * (k + 1)]
+                    src = raw[("x", k)][:, 0 : C // 2 * NPIX].rearrange("b (c l) -> b c l", l=NPIX)
+                    src = src[:, :, 4 * a : 4 * a + 4]
+                else:
+                    h, w = locs[k]
+                    i0, j0, nj = valid(h)[a], valid(w)[0], len(valid(w))
+                    cs = slice(q * C // pieces, (q + 1) * C // pieces)
+                    src = raw[("w", k)][:].rearrange("o (c i j) -> o c i j", i=KK, j=KK)
+                    out_cols = d[:, a * nj * C : (a + ni) * nj * C]
+                    if ni == 2:
+                        dst = out_cols.rearrange("o (i j c) -> o c i j", i=2, j=2)[:, cs]
+                        src = src[:, cs, i0 : i0 + 2, j0 : j0 + 2]
+                    else:
+                        dst = out_cols.rearrange("o (s c) -> o c s", c=C)[:, cs]
+                        src = src[:, cs, i0, j0 : j0 + nj]
+                if on_scalar(kind, k, a, n):
+                    nc.scalar.copy(out=dst, in_=src)
+                else:
+                    nc.vector.tensor_copy(out=dst, in_=src)
+                done_jobs[0] = n + 1
+                if n + 1 == len(jobs) or jobs[n + 1][0:2] != (kind, k):
+                    load_next()
+
+        def on_scalar(kind, unit, a, n):
+            return (kind == "w" and unit == 0 and a == 1) or (kind == "w" and a == 1 or kind == "x" and a == 3)
 
         g_of = {}
-        q_of = {}
-        acc_of = {}
-        group_of_bank = []
-        for gi, grp in enumerate(groups):
-            for bk in range(len(grp) // 2):
-                group_of_bank.append((gi, bk))
 
-        def w_bank(b):
-            gi, bk = group_of_bank[b]
-            grp = groups[gi]
+        def transpose_bank(key, size, bk, sources, b):
             if bk == 0:
-                g_of[gi] = gpool.tile([P, GROUP * C], BF16, tag="g", name="g%d" % gi, align_bytes=64)
-            ps = tpool.tile([P, 512], F32, tag="tp", name="pw%d_%d" % (gi, bk))
-            for t in range(2):
-                tap = grp[2 * bk + t]
-                d32 = d_of[tap[0]][:].bitcast(F32)
+                g_of[key] = gpool.tile([P, GROUP * C], BF16, tag="g", name="g_%s%d" % key, align_bytes=64)
+            ps = tpool.tile([P, 512], F32, tag="tp", name="ps_%s%d_%d" % (key[0], key[1], bk))
+            for t, (d, s) in enumerate(sources):
+                words = d[:].bitcast(F32)[:, s * 256 : (s + 1) * 256]
                 for u in range(2):
-                    nc.tensor.transpose(
-                        ps[:, (2 * t + u) * P : (2 * t + u + 1) * P],
-                        d32[:, tap[5] * 256 + u : tap[5] * 256 + 256 : 2],
-                        ident[:],
-                    )
-            (nc.vector.tensor_copy if copy_on_vector(b) else nc.scalar.copy)(
-                out=g_of[gi][:].bitcast(F32)[:, 512 * bk : 512 * (bk + 1)].rearrange("p (t o u) -> p t o u", t=2, u=2),
+                    nc.tensor.transpose(ps[:, (2 * t + u) * P : (2 * t + u + 1) * P], words[:, u:256:2], ident[:])
+            (nc.vector.tensor_copy if False else nc.scalar.copy)(
+                out=g_of[key][:].bitcast(F32)[:, 512 * bk : 512 * (bk + 1)].rearrange("p (t o u) -> p t o u", t=2, u=2),
                 in_=ps[:].rearrange("p (t u o) -> p t o u", t=2, u=2),
             )
 
-        def stage_q(gi):
+        def quantise_x(xg):
+            cols = slice(xg * XGROUP * B, (xg + 1) * XGROUP * B)
+            nc.vector.quantize_mx(
+                out=xq[:, cols].bitcast(FP8X4), scales=xs[:, cols], in_=g_of[("x", xg)][:, 0 : XGROUP * C]
+            )
+
+        q_of = {}
+
+        def quantise_w(gi):
             wq = qpool.tile([P, GROUP * O], U32, tag="wq", name="wq%d" % gi, align_bytes=64)
             ws = qpool.tile([P, GROUP * O], U8, tag="ws", name="ws%d" % gi, align_bytes=64)
             n = len(groups[gi])
             nc.vector.quantize_mx(
-                out=wq[:, 0 : n * O].bitcast(FP8X4), scales=ws[:, 0 : n * O], in_=g_of[gi][:, 0 : n * C]
+                out=wq[:, 0 : n * O].bitcast(FP8X4), scales=ws[:, 0 : n * O], in_=g_of[("w", gi)][:, 0 : n * C]
             )
             q_of[gi] = (wq, ws)
 
@@ -239,7 +240,9 @@ def tile_locallyconnected2d_kernel(tc, x, weights, bias, out):
                         in_=result[:, q * step * NPIX : (q + 1) * step * NPIX],
                     )
 
-        def stage_m(gi):
+        acc_of = {}
+
+        def multiply(gi):
             wq, ws = q_of[gi]
             for n, (k, h, w, i, j, s, first, last) in enumerate(groups[gi]):
                 if w == COL_ORDER[0] and first:
@@ -258,44 +261,38 @@ def tile_locallyconnected2d_kernel(tc, x, weights, bias, out):
                 if w == COL_ORDER[-1] and last:
                     finish_row(h, acc)
 
-        nb = len(group_of_bank)
-        steps = []
-        for b in range(nb):
-            for r in range(2 * NPIX // XGROUP):
-                if b == X_AT + r * X_STRIDE:
-                    steps.append(("x", r))
-            steps.append(("w", b))
-        due_q = []
-        due_m = []
-        x_ready = False
-        t = 0
-        b = 0
-        extra = 0
-        while t < len(steps) or due_q or due_m:
-            if t < len(steps):
-                kind, n = steps[t]
-                if kind == "w":
-                    b = n
+        due = []
+        waiting = []
+        x_left = NPIX // XGROUP
+        at = 0
+        while at < len(steps) or due or waiting:
+            if at < len(steps):
+                sort_up_to(at + LOOKAHEAD, at)
+                kind, n = steps[at]
+                if kind == "x":
+                    xg, bk = divmod(n, XGROUP // 2)
+                    d = d_of[("x", n // (n_xbanks // 2))]
+                    s = 2 * (n % (n_xbanks // 2))
+                    transpose_bank(("x", xg), XGROUP, bk, [(d, s), (d, s + 1)], n)
+                    if bk == XGROUP // 2 - 1:
+                        due.append((at + XQ_LAG, "xq", xg))
                 else:
-                    extra += 1
-                sort_up_to(2 * (b + 1 + LOOKAHEAD) + extra, b)
-                if kind == "w":
-                    w_bank(n)
-                    gi, bk = group_of_bank[n]
+                    gi, bk = banks[n]
+                    pair = groups[gi][2 * bk : 2 * bk + 2]
+                    transpose_bank(("w", gi), len(groups[gi]), bk, [(d_of[("w", tap[0])], tap[5]) for tap in pair], n)
                     if 2 * bk + 2 == len(groups[gi]):
-                        due_q.append((t + Q_LAG, "w", gi))
-                        due_m.append((t + M_LAG, gi))
-                else:
-                    x_bank(n)
-                    if n % 2 == 1:
-                        due_q.append((t + XQ_LAG, "x", n // 2))
-            for job in sorted(due_q):
-                if job[0] <= t:
-                    due_q.remove(job)
-                    fn = stage_q if job[1] == "w" else quantise_x
-                    fn(job[2])
-                    if job[1] == "x" and job[2] == NPIX // XGROUP - 1:
-                        x_ready = True
-            while due_m and due_m[0][0] <= t and x_ready:
-                stage_m(due_m.pop(0)[1])
-            t += 1
+                        due.append((at + Q_LAG, "wq", gi))
+                        due.append((at + M_LAG, "m", gi))
+            for job in sorted(due):
+                if job[0] <= at:
+                    due.remove(job)
+                    if job[1] == "xq":
+                        quantise_x(job[2])
+                        x_left -= 1
+                    elif job[1] == "wq":
+                        quantise_w(job[2])
+                    else:
+                        waiting.append(job[2])
+            while waiting and x_left == 0:
+                multiply(waiting.pop(0))
+            at += 1

@@ -23,22 +23,25 @@ ROW_ORDER = (1, 2, 0, 3)
 COL_ORDER = (1, 2, 0, 3)
 GROUP = 8
 LAST_GROUP = 4
-N_COARSE = 72
+N_TAIL = 4
+TAIL_GROUP = 2
+N_COARSE = 64
 XGROUP = 4
 W_FIRST = 1
 X_AT = 4
 X_STRIDE = 0
-PIECES = {0: 2}
-LOOKAHEAD = 4
-Q_LAG = 1
-XQ_LAG = 4
-M_LAG = 8
+X_PIECES = 1
+PIECES = {0: 2, 15: 2}
+LOOKAHEAD = 5
+Q_LAG = 2
+XQ_LAG = 5
+M_LAG = 9
 LOAD_BUFS = 7
-D_BUFS = 7
-G_BUFS = 4
-Q_BUFS = 6
+D_BUFS = 6
+G_BUFS = 5
+Q_BUFS = 7
 TP_BUFS = 6
-STORE_CUTS = 4
+STORE_CUTS = 8
 
 
 def valid(p):
@@ -67,10 +70,13 @@ def tile_locallyconnected2d_kernel(tc, x, weights, bias, out):
                 kind, k = unit
                 t = loads.tile([P, ROW], BF16, tag="ld", name="raw_%s%d" % unit)
                 if kind == "x":
-                    nc.sync.dma_start(
-                        out=t[:, 0 : C // 2 * NPIX],
-                        in_=x[:, C // 2 * k : C // 2 * (k + 1)].rearrange("b c y x -> b (c y x)"),
-                    )
+                    part = C // 2 // X_PIECES
+                    for q in range(X_PIECES):
+                        first = C // 2 * k + part * q
+                        nc.sync.dma_start(
+                            out=t[:, part * NPIX * q : part * NPIX * (q + 1)],
+                            in_=x[:, first : first + part].rearrange("b c y x -> b (c y x)"),
+                        )
                 else:
                     h, w = locs[k]
                     rows = weights[h, w].rearrange("o c i j -> o (c i j)")
@@ -97,7 +103,8 @@ def tile_locallyconnected2d_kernel(tc, x, weights, bias, out):
             for s, (i, j) in enumerate(lst):
                 taps.append((k, h, w, i, j, s, s == 0, s == len(lst) - 1))
         groups = [taps[a : a + GROUP] for a in range(0, N_COARSE, GROUP)]
-        groups += [taps[a : a + LAST_GROUP] for a in range(N_COARSE, len(taps), LAST_GROUP)]
+        groups += [taps[a : a + LAST_GROUP] for a in range(N_COARSE, len(taps) - N_TAIL, LAST_GROUP)]
+        groups += [taps[a : a + TAIL_GROUP] for a in range(len(taps) - N_TAIL, len(taps), TAIL_GROUP)]
         banks = [(gi, bk) for gi, grp in enumerate(groups) for bk in range(len(grp) // 2)]
         n_xbanks = NPIX // 2
         steps = []
@@ -122,8 +129,9 @@ def tile_locallyconnected2d_kernel(tc, x, weights, bias, out):
         jobs = []
         for kind, k in order:
             if kind == "x":
-                for quad in range(4):
-                    jobs.append(("x", k, quad, 4, 0, 1))
+                for q in range(X_PIECES):
+                    for quad in range(4):
+                        jobs.append(("x", k, quad, 4, q, X_PIECES))
             else:
                 rows_i, nj = valid(locs[k][0]), len(valid(locs[k][1]))
                 ni = 2 if nj == 2 else 1
@@ -161,9 +169,10 @@ def tile_locallyconnected2d_kernel(tc, x, weights, bias, out):
                     return
                 if kind == "x":
                     dst = d[:, 4 * C * (a % 2) : 4 * C * (a % 2 + 1)].rearrange("b (l c) -> b c l", c=C)
-                    dst = dst[:, C // 2 * k : C // 2 * (k + 1)]
+                    part = C // 2 // pieces
+                    dst = dst[:, C // 2 * k + part * q : C // 2 * k + part * (q + 1)]
                     src = raw[("x", k)][:, 0 : C // 2 * NPIX].rearrange("b (c l) -> b c l", l=NPIX)
-                    src = src[:, :, 4 * a : 4 * a + 4]
+                    src = src[:, part * q : part * (q + 1), 4 * a : 4 * a + 4]
                 else:
                     h, w = locs[k]
                     i0, j0, nj = valid(h)[a], valid(w)[0], len(valid(w))

@@ -25,17 +25,18 @@ GROUP = 8
 LAST_GROUP = 4
 N_TAIL = 4
 TAIL_GROUP = 2
-N_COARSE = 64
+N_COARSE = 48
 XGROUP = 4
 W_FIRST = 1
 X_AT = 4
 X_STRIDE = 0
-X_PIECES = 1
+X_PIECES = 2
 PIECES = {0: 2, 15: 2}
-LOOKAHEAD = 5
+LOOKAHEAD = 3
 Q_LAG = 2
-XQ_LAG = 5
-M_LAG = 9
+XQ_LAG = 7
+M_LAG = 8
+ADD_LAG = 4
 LOAD_BUFS = 7
 D_BUFS = 6
 G_BUFS = 5
@@ -194,7 +195,7 @@ def tile_locallyconnected2d_kernel(tc, x, weights, bias, out):
                     load_next()
 
         def on_scalar(kind, unit, a, n):
-            return (kind == "w" and unit == 0 and a == 1) or (kind == "w" and a == 1 or kind == "x" and a == 3)
+            return (kind == "w" and unit == 0 and a == 1) or (kind == "w" and (a == 1 and unit > 1) or kind == "x" and a == 3)
 
         g_of = {}
 
@@ -251,7 +252,7 @@ def tile_locallyconnected2d_kernel(tc, x, weights, bias, out):
 
         acc_of = {}
 
-        def multiply(gi):
+        def multiply(gi, at):
             wq, ws = q_of[gi]
             for n, (k, h, w, i, j, s, first, last) in enumerate(groups[gi]):
                 if w == COL_ORDER[0] and first:
@@ -268,7 +269,10 @@ def tile_locallyconnected2d_kernel(tc, x, weights, bias, out):
                     stop=last,
                 )
                 if w == COL_ORDER[-1] and last:
-                    finish_row(h, acc)
+                    if h == ROW_ORDER[-1]:
+                        finish_row(h, acc)
+                    else:
+                        due.append((at + ADD_LAG, "z", h))
 
         due = []
         waiting = []
@@ -300,8 +304,10 @@ def tile_locallyconnected2d_kernel(tc, x, weights, bias, out):
                         x_left -= 1
                     elif job[1] == "wq":
                         quantise_w(job[2])
+                    elif job[1] == "z":
+                        finish_row(job[2], acc_of[job[2]])
                     else:
                         waiting.append(job[2])
             while waiting and x_left == 0:
-                multiply(waiting.pop(0))
+                multiply(waiting.pop(0), at)
             at += 1

@@ -42,7 +42,7 @@ D_BUFS = 6
 G_BUFS = 5
 Q_BUFS = 7
 TP_BUFS = 6
-STORE_CUTS = 8
+STORE_CUTS = 4
 
 
 def valid(p):

from contextlib import ExitStack

import concourse.mybir as mybir
from concourse.masks import make_identity

BF16 = mybir.dt.bfloat16
F32 = mybir.dt.float32
U32 = mybir.dt.uint32
U8 = mybir.dt.uint8
FP8X4 = mybir.dt.float8_e4m3fn_x4

P = 128
B = 128
C = 512
O = 128
HW = 4
KK = 3
NPIX = HW * HW
ROW = C * KK * KK
FLOPS = 2 * 100 * B * O * C

ROW_ORDER = (1, 2, 0, 3)
COL_ORDER = (1, 2, 0, 3)
GROUP = 8
LAST_GROUP = 4
N_TAIL = 4
TAIL_GROUP = 2
N_COARSE = 48
XGROUP = 4
W_FIRST = 1
X_AT = 4
X_STRIDE = 0
X_PIECES = 2
PIECES = {0: 2, 15: 2}
LOOKAHEAD = 3
Q_LAG = 2
XQ_LAG = 7
M_LAG = 8
ADD_LAG = 4
LOAD_BUFS = 7
D_BUFS = 6
G_BUFS = 5
Q_BUFS = 7
TP_BUFS = 6
STORE_CUTS = 4


def valid(p):
    return [t for t in range(KK) if 0 <= p + t - 1 < HW]


def tile_locallyconnected2d_kernel(tc, x, weights, bias, out):
    nc = tc.nc
    with ExitStack() as ctx:
        ctx.enter_context(tc.manual_schedule())
        const = ctx.enter_context(tc.tile_pool(name="const", bufs=1))
        loads = ctx.enter_context(tc.tile_pool(name="loads", bufs=LOAD_BUFS))
        dpool = ctx.enter_context(tc.tile_pool(name="dpool", bufs=D_BUFS))
        gpool = ctx.enter_context(tc.tile_pool(name="gpool", bufs=G_BUFS))
        qpool = ctx.enter_context(tc.tile_pool(name="qpool", bufs=Q_BUFS))
        tpool = ctx.enter_context(tc.psum_pool(name="tpool", bufs=TP_BUFS))
        apool = ctx.enter_context(tc.psum_pool(name="apool", bufs=2))

        locs = [(h, w) for h in ROW_ORDER for w in COL_ORDER]
        order = [("w", k) for k in range(W_FIRST)] + [("x", 0), ("x", 1)] + [("w", k) for k in range(W_FIRST, len(locs))]
        raw = {}

        def load_next():
            if len(raw) < len(order):
                unit = order[len(raw)]
                kind, k = unit
                t = loads.tile([P, ROW], BF16, tag="ld", name="raw_%s%d" % unit)
                if kind == "x":
                    part = C // 2 // X_PIECES
                    for q in range(X_PIECES):
                        first = C // 2 * k + part * q
                        nc.sync.dma_start(
                            out=t[:, part * NPIX * q : part * NPIX * (q + 1)],
                            in_=x[:, first : first + part].rearrange("b c y x -> b (c y x)"),
                        )
                else:
                    h, w = locs[k]
                    rows = weights[h, w].rearrange("o c i j -> o (c i j)")
                    n = PIECES.get(k, 1)
                    for q in range(n):
                        cols = slice(q * ROW // n, (q + 1) * ROW // n)
                        nc.sync.dma_start(out=t[:, cols], in_=rows[:, cols])
                raw[unit] = t

        for n in range(LOAD_BUFS):
            load_next()

        ident = const.tile([P, P], F32, name="ident")
        make_identity(nc, ident[:])
        bias_all = const.tile([P, O * NPIX], BF16, name="bias_all")
        nc.sync.dma_start(out=bias_all[:], in_=bias.rearrange("o y x -> (o y x)").partition_broadcast(P))
        result = const.tile([P, O * NPIX], F32, name="result")
        xq = const.tile([P, NPIX * B], U32, name="xq", align_bytes=64)
        xs = const.tile([P, NPIX * B], U8, name="xs", align_bytes=64)

        taps = []
        for k, (h, w) in enumerate(locs):
            lst = [(i, j) for i in valid(h) for j in valid(w)]
            for s, (i, j) in enumerate(lst):
                taps.append((k, h, w, i, j, s, s == 0, s == len(lst) - 1))
        groups = [taps[a : a + GROUP] for a in range(0, N_COARSE, GROUP)]
        groups += [taps[a : a + LAST_GROUP] for a in range(N_COARSE, len(taps) - N_TAIL, LAST_GROUP)]
        groups += [taps[a : a + TAIL_GROUP] for a in range(len(taps) - N_TAIL, len(taps), TAIL_GROUP)]
        banks = [(gi, bk) for gi, grp in enumerate(groups) for bk in range(len(grp) // 2)]
        n_xbanks = NPIX // 2
        steps = []
        for b in range(len(banks)):
            for r in range(n_xbanks):
                if b == X_AT + r * X_STRIDE:
                    steps.append(("x", r))
            steps.append(("w", b))

        first_use = {}
        last_use = {}
        for at, (kind, n) in enumerate(steps):
            if kind == "x":
                units = [("x", n // (n_xbanks // 2))]
            else:
                gi, bk = banks[n]
                units = [("w", tap[0]) for tap in groups[gi][2 * bk : 2 * bk + 2]]
            for unit in units:
                first_use.setdefault(unit, at)
                last_use[unit] = at

        jobs = []
        for kind, k in order:
            if kind == "x":
                for q in range(X_PIECES):
                    for quad in range(4):
                        jobs.append(("x", k, quad, 4, q, X_PIECES))
            else:
                rows_i, nj = valid(locs[k][0]), len(valid(locs[k][1]))
                ni = 2 if nj == 2 else 1
                n = PIECES.get(k, 1)
                for q in range(n):
                    for a in range(0, len(rows_i), ni):
                        jobs.append(("w", k, a, min(ni, len(rows_i) - a), q, n))

        def need(job):
            kind, k, a, ni, q, n = job
            return first_use[("x", a // 2) if kind == "x" else ("w", k)]

        d_of = {}
        d_units = []

        def sorted_tile(unit, at):
            if unit not in d_of:
                if len(d_units) >= D_BUFS and last_use[d_units[len(d_units) - D_BUFS]] >= at:
                    return None
                d_of[unit] = dpool.tile([P, ROW], BF16, tag="d", name="d_%s%d" % unit)
                d_units.append(unit)
            return d_of[unit]

        done_jobs = [0]

        def sort_up_to(limit, at):
            while done_jobs[0] < len(jobs):
                n = done_jobs[0]
                if min(need(job) for job in jobs[n:]) > limit:
                    return
                kind, k, a, ni, q, pieces = jobs[n]
                unit = ("x", a // 2) if kind == "x" else ("w", k)
                d = sorted_tile(unit, at)
                if d is None:
                    return
                if kind == "x":
                    dst = d[:, 4 * C * (a % 2) : 4 * C * (a % 2 + 1)].rearrange("b (l c) -> b c l", c=C)
                    part = C // 2 // pieces
                    dst = dst[:, C // 2 * k + part * q : C // 2 * k + part * (q + 1)]
                    src = raw[("x", k)][:, 0 : C // 2 * NPIX].rearrange("b (c l) -> b c l", l=NPIX)
                    src = src[:, part * q : part * (q + 1), 4 * a : 4 * a + 4]
                else:
                    h, w = locs[k]
                    i0, j0, nj = valid(h)[a], valid(w)[0], len(valid(w))
                    cs = slice(q * C // pieces, (q + 1) * C // pieces)
                    src = raw[("w", k)][:].rearrange("o (c i j) -> o c i j", i=KK, j=KK)
                    out_cols = d[:, a * nj * C : (a + ni) * nj * C]
                    if ni == 2:
                        dst = out_cols.rearrange("o (i j c) -> o c i j", i=2, j=2)[:, cs]
                        src = src[:, cs, i0 : i0 + 2, j0 : j0 + 2]
                    else:
                        dst = out_cols.rearrange("o (s c) -> o c s", c=C)[:, cs]
                        src = src[:, cs, i0, j0 : j0 + nj]
                if on_scalar(kind, k, a, n):
                    nc.scalar.copy(out=dst, in_=src)
                else:
                    nc.vector.tensor_copy(out=dst, in_=src)
                done_jobs[0] = n + 1
                if n + 1 == len(jobs) or jobs[n + 1][0:2] != (kind, k):
                    load_next()

        def on_scalar(kind, unit, a, n):
            return (kind == "w" and unit == 0 and a == 1) or (kind == "w" and (a == 1 and unit > 1) or kind == "x" and a == 3)

        g_of = {}

        def transpose_bank(key, size, bk, sources, b):
            if bk == 0:
                g_of[key] = gpool.tile([P, GROUP * C], BF16, tag="g", name="g_%s%d" % key, align_bytes=64)
            ps = tpool.tile([P, 512], F32, tag="tp", name="ps_%s%d_%d" % (key[0], key[1], bk))
            for t, (d, s) in enumerate(sources):
                words = d[:].bitcast(F32)[:, s * 256 : (s + 1) * 256]
                for u in range(2):
                    nc.tensor.transpose(ps[:, (2 * t + u) * P : (2 * t + u + 1) * P], words[:, u:256:2], ident[:])
            (nc.vector.tensor_copy if False else nc.scalar.copy)(
                out=g_of[key][:].bitcast(F32)[:, 512 * bk : 512 * (bk + 1)].rearrange("p (t o u) -> p t o u", t=2, u=2),
                in_=ps[:].rearrange("p (t u o) -> p t o u", t=2, u=2),
            )

        def quantise_x(xg):
            cols = slice(xg * XGROUP * B, (xg + 1) * XGROUP * B)
            nc.vector.quantize_mx(
                out=xq[:, cols].bitcast(FP8X4), scales=xs[:, cols], in_=g_of[("x", xg)][:, 0 : XGROUP * C]
            )

        q_of = {}

        def quantise_w(gi):
            wq = qpool.tile([P, GROUP * O], U32, tag="wq", name="wq%d" % gi, align_bytes=64)
            ws = qpool.tile([P, GROUP * O], U8, tag="ws", name="ws%d" % gi, align_bytes=64)
            n = len(groups[gi])
            nc.vector.quantize_mx(
                out=wq[:, 0 : n * O].bitcast(FP8X4), scales=ws[:, 0 : n * O], in_=g_of[("w", gi)][:, 0 : n * C]
            )
            q_of[gi] = (wq, ws)

        res3 = result[:].rearrange("b (o l) -> b o l", l=NPIX)
        bias3 = bias_all[:].rearrange("b (o l) -> b o l", l=NPIX)
        out2 = out.rearrange("b o y x -> b (o y x)")

        def finish_row(h, acc):
            acc3 = acc[:].rearrange("b (w o) -> b o w", w=HW)
            cuts = STORE_CUTS if h == ROW_ORDER[-1] else 1
            step = O // cuts
            for q in range(cuts):
                nc.vector.tensor_tensor(
                    out=res3[:, q * step : (q + 1) * step, HW * h : HW * (h + 1)],
                    in0=acc3[:, q * step : (q + 1) * step, :],
                    in1=bias3[:, q * step : (q + 1) * step, HW * h : HW * (h + 1)],
                    op=mybir.AluOpType.add,
                )
                if h == ROW_ORDER[-1]:
                    nc.sync.dma_start(
                        out=out2[:, q * step * NPIX : (q + 1) * step * NPIX],
                        in_=result[:, q * step * NPIX : (q + 1) * step * NPIX],
                    )

        acc_of = {}

        def multiply(gi, at):
            wq, ws = q_of[gi]
            for n, (k, h, w, i, j, s, first, last) in enumerate(groups[gi]):
                if w == COL_ORDER[0] and first:
                    acc_of[h] = apool.tile([P, 512], F32, tag="acc", name="acc%d" % h)
                acc = acc_of[h]
                pix = (h + i - 1) * HW + (w + j - 1)
                nc.tensor.matmul_mx(
                    out=acc[:, w * O : (w + 1) * O],
                    lhsT=xq[:, pix * B : (pix + 1) * B].bitcast(FP8X4),
                    lhsT_scale=xs[:, pix * B : (pix + 1) * B],
                    rhs=wq[:, n * O : (n + 1) * O].bitcast(FP8X4),
                    rhs_scale=ws[:, n * O : (n + 1) * O],
                    start=first,
                    stop=last,
                )
                if w == COL_ORDER[-1] and last:
                    if h == ROW_ORDER[-1]:
                        finish_row(h, acc)
                    else:
                        due.append((at + ADD_LAG, "z", h))

        due = []
        waiting = []
        x_left = NPIX // XGROUP
        at = 0
        while at < len(steps) or due or waiting:
            if at < len(steps):
                sort_up_to(at + LOOKAHEAD, at)
                kind, n = steps[at]
                if kind == "x":
                    xg, bk = divmod(n, XGROUP // 2)
                    d = d_of[("x", n // (n_xbanks // 2))]
                    s = 2 * (n % (n_xbanks // 2))
                    transpose_bank(("x", xg), XGROUP, bk, [(d, s), (d, s + 1)], n)
                    if bk == XGROUP // 2 - 1:
                        due.append((at + XQ_LAG, "xq", xg))
                else:
                    gi, bk = banks[n]
                    pair = groups[gi][2 * bk : 2 * bk + 2]
                    transpose_bank(("w", gi), len(groups[gi]), bk, [(d_of[("w", tap[0])], tap[5]) for tap in pair], n)
                    if 2 * bk + 2 == len(groups[gi]):
                        due.append((at + Q_LAG, "wq", gi))
                        due.append((at + M_LAG, "m", gi))
            for job in sorted(due):
                if job[0] <= at:
                    due.remove(job)
                    if job[1] == "xq":
                        quantise_x(job[2])
                        x_left -= 1
                    elif job[1] == "wq":
                        quantise_w(job[2])
                    elif job[1] == "z":
                        finish_row(job[2], acc_of[job[2]])
                    else:
                        waiting.append(job[2])
            while waiting and x_left == 0:
                multiply(waiting.pop(0), at)
            at += 1
